import numpy as np
import ml_dtypes


def mxq(x, axis, fmt="e4m3"):
    dtype, down = {"e4m3": (ml_dtypes.float8_e4m3fn, 7), "e5m2": (ml_dtypes.float8_e5m2, 14)}[fmt]
    v = np.moveaxis(np.asarray(x, np.float32).astype(ml_dtypes.bfloat16).astype(np.float64), axis, -1)
    blocks = v.reshape(v.shape[:-1] + (-1, 32))
    amax = np.abs(blocks).max(-1, keepdims=True)
    byte = np.maximum(np.where(amax > 0, np.frexp(amax)[1] - 1 + 127, 0) - down, 1)
    scale = np.exp2(byte - 127.0)
    codes = (blocks / scale).astype(np.float32).astype(dtype).astype(np.float64)
    return np.moveaxis((codes * scale).reshape(v.shape), -1, axis)


WIDE = False


def mx_kscale(k):
    if not WIDE:
        return np.ones(k)
    levels = np.array([10, -10, 5, -5, 0])
    if k % 512:
        return np.exp2(np.random.permutation(np.resize(levels, k // 32))).repeat(32)
    a = np.empty((k // 512, 16))
    for p in range(k // 512):
        a[p, :8] = np.random.permutation(np.resize(levels, 8))
        for g in range(8):
            far = levels[np.abs(levels - a[p, g]) >= 10]
            a[p, g + 8] = far[np.random.randint(len(far))]
    return np.exp2(a.ravel()).repeat(32)


BF16 = ml_dtypes.bfloat16


def bf(x):
    return np.asarray(x, np.float32).astype(BF16)


def f64(x):
    return np.asarray(x).astype(np.float64)


B, D, HID, G0, RIN, NR = 256, 1024, 2048, 512, 256, 5
EPS = 1e-05
W2S = 0.02


def silu(v):
    return v / (1.0 + np.exp(-v))


def draw0():
    s, t = mx_kscale(G0), mx_kscale(HID)
    return {"x0": bf(np.random.standard_normal((B, G0)) * s),
            "w1_g0": bf(np.random.standard_normal((HID, G0)) / np.sqrt(G0) / s),
            "w3_g0": bf(np.random.standard_normal((HID, G0)) / np.sqrt(G0) / s * t[:, None]),
            "w2_g0": bf(np.random.standard_normal((D, HID)) * W2S / np.sqrt(HID) / t),
            "norm_w": bf(1.0 + 0.1 * np.random.standard_normal(D)),
            "norm_b": bf(0.1 * np.random.standard_normal(D)),
            "term_embed0": bf(np.random.standard_normal(D))}


def core(x0, w1_g0, w3_g0, w2_g0, norm_w, norm_b, term_embed0):
    xq = mxq(f64(x0), 1, "e4m3")
    gate0 = silu(xq @ mxq(f64(w1_g0), 1, "e4m3").T)
    h = gate0 * (xq @ mxq(f64(w3_g0), 1, "e4m3").T)
    tok = mxq(h, 1, "e4m3") @ mxq(f64(w2_g0), 1, "e4m3").T
    rms = np.sqrt(np.mean(tok * tok, axis=-1, keepdims=True) + EPS)
    return (tok / rms) * f64(norm_w) + f64(norm_b) + f64(term_embed0)


def e4m3fn_bytes(y):
    return np.clip(np.asarray(y, np.float64), -448.0, 448.0).astype(np.float32).astype(ml_dtypes.float8_e4m3fn).view(np.uint8)


def e4m3fn_values(b):
    return np.asarray(b, np.uint8).view(ml_dtypes.float8_e4m3fn).astype(np.float64)


def setup_inputs():
    d = draw0()
    x0 = np.asarray(d['w2_g0']).astype(np.float64)
    s = (np.max(np.abs(x0), axis=(0,), keepdims=True) / 448.0).astype(np.float32)
    out = {}
    for k, v in d.items():
        if k == 'w2_g0':
            out['w2_g0_bytes'] = e4m3fn_bytes(x0 / s.astype(np.float64))
            out['w2_g0_scale'] = s
        else:
            out[k] = v
    return out


def reference(x0, w1_g0, w3_g0, w2_g0_bytes, w2_g0_scale, norm_w, norm_b, term_embed0):
    return core(x0, w1_g0, w3_g0, e4m3fn_values(w2_g0_bytes) * w2_g0_scale.astype(np.float64), norm_w, norm_b, term_embed0)

@@ -1,0 +1,308 @@
+from contextlib import ExitStack
+
+import concourse.mybir as mybir
+from concourse.masks import make_identity
+
+B, G0, HID, D = 256, 512, 2048, 1024
+EPS = 1e-5
+FLOPS = 2 * B * G0 * HID * 2 + 2 * B * HID * D
+
+F32 = mybir.dt.float32
+BF16 = mybir.dt.bfloat16
+U32 = mybir.dt.uint32
+U8 = mybir.dt.uint8
+FP8 = mybir.dt.float8_e4m3fn
+FP8X4 = mybir.dt.float8_e4m3fn_x4
+MULT = mybir.AluOpType.mult
+ADD = mybir.AluOpType.add
+ACT = mybir.ActivationFunctionType
+
+P = 128
+PACK = 4
+K_PASS = P * PACK
+GROUPS = HID // K_PASS
+ROW_TILES = D // P
+TOKEN_TILES = B // P
+HALF = HID // 2
+
+
+def tile_observationembeddingv2_pa_kernel(
+    tc, x0, w1_g0, w3_g0, w2_g0_bytes, w2_g0_scale, norm_w, norm_b, term_embed0, out
+):
+    nc = tc.nc
+    with ExitStack() as ctx:
+        keep = ctx.enter_context(tc.tile_pool(name="keep", bufs=1))
+        work = ctx.enter_context(tc.tile_pool(name="work", bufs=6))
+        psum = ctx.enter_context(tc.psum_pool(name="psum", bufs=4))
+        ctx.enter_context(tc.manual_schedule())
+
+        x_raw = keep.tile([P, TOKEN_TILES, G0], BF16, name="x_raw", align_bytes=64)
+        w_raw = {}
+        for g in range(GROUPS):
+            for w in (0, 1):
+                w_raw[w, g] = keep.tile([P, PACK, G0], BF16, name=f"w_raw_{w}_{g}", align_bytes=64)
+        byte_tiles = [keep.tile([P, HID], U8, name=f"byte_tile_{r}", align_bytes=64) for r in range(ROW_TILES)]
+        scaled = [keep.tile([P, HID], BF16, name=f"scaled_{r}", align_bytes=64) for r in range(ROW_TILES)]
+        scale_all = keep.tile([P, HID], F32, name="scale_all", align_bytes=64)
+        gain = keep.tile([P, D], BF16, name="gain", align_bytes=64)
+        bias_rows = keep.tile([P, D], BF16, name="bias_rows", align_bytes=64)
+        ones = keep.tile([P, P], BF16, name="ones", align_bytes=64)
+        bias = keep.tile([P, D], F32, name="bias", align_bytes=64)
+        ident = keep.tile([P, P], F32, name="ident", align_bytes=64)
+        dummy = keep.tile([P, 1], F32, name="dummy")
+        dummy_out = keep.tile([P, 1], F32, name="dummy_out")
+        square_out = keep.tile([P, 512], F32, name="square_out", align_bytes=64)
+
+        def load_scale(g):
+            nc.sync.dma_start(
+                out=scale_all[:, g * K_PASS : (g + 1) * K_PASS],
+                in_=w2_g0_scale.rearrange("o k -> (o k)")[g * K_PASS : (g + 1) * K_PASS].partition_broadcast(P),
+            )
+
+        def load_bytes(r):
+            nc.sync.dma_start(out=byte_tiles[r][:], in_=w2_g0_bytes[r * P : (r + 1) * P, :])
+
+        def load_w(w, g):
+            source = (w1_g0, w3_g0)[w][g * K_PASS : (g + 1) * K_PASS, :]
+            nc.sync.dma_start(out=w_raw[w, g][:], in_=source.rearrange("(m t) k -> m t k", t=PACK))
+
+        load_scale(0)
+        load_bytes(0)
+        nc.sync.dma_start(out=x_raw[:], in_=x0.rearrange("(a p) k -> p a k", p=P))
+        load_scale(1)
+        load_bytes(1)
+        load_w(0, 0)
+        load_scale(2)
+        load_scale(3)
+        load_w(1, 0)
+        load_bytes(2)
+        load_w(0, 1)
+        load_w(1, 1)
+        load_bytes(3)
+        load_w(0, 2)
+        load_w(1, 2)
+        load_bytes(4)
+        load_w(0, 3)
+        load_w(1, 3)
+        for r in range(5, ROW_TILES):
+            load_bytes(r)
+        nc.sync.dma_start(out=gain[:], in_=norm_w.partition_broadcast(P))
+
+        make_identity(nc, ident[:])
+        nc.gpsimd.memset(bias_rows[:], 0.0)
+        nc.gpsimd.memset(ones[:], 1.0)
+        nc.vector.memset(dummy[:], 0.0)
+        nc.scalar.dma_start(out=bias_rows[0:1, :], in_=norm_b.rearrange("(o d) -> o d", o=1))
+        nc.scalar.dma_start(out=bias_rows[1:2, :], in_=term_embed0.rearrange("(o d) -> o d", o=1))
+        nc.scalar.activation(out=dummy_out[:], in_=dummy[:], func=ACT.Silu)
+
+        def operand(name, width):
+            return (
+                keep.tile([P, width], U32, name=name + "_codes", align_bytes=64),
+                keep.tile([P, width], U8, name=name + "_scales", align_bytes=64),
+            )
+
+        x_op = operand("x", B)
+        w_op = {(w, g): operand(f"w_{w}_{g}", K_PASS) for w in (0, 1) for g in range(GROUPS)}
+        h_op = [operand(f"h_{g}", B) for g in range(GROUPS)]
+        w2_op = [operand(f"w2_{r}", K_PASS) for r in range(ROW_TILES)]
+
+        def quantize(op, values):
+            nc.vector.quantize_mx(out=op[0][:].bitcast(FP8X4), scales=op[1][:], in_=values[:].rearrange("p c j -> p (c j)"))
+
+        def mx(acc, lhs, lhs_cols, rhs, rhs_cols, start, stop):
+            nc.tensor.matmul_mx(
+                out=acc,
+                lhsT=lhs[0][:, lhs_cols].bitcast(FP8X4),
+                lhsT_scale=lhs[1][:, lhs_cols],
+                rhs=rhs[0][:, rhs_cols].bitcast(FP8X4),
+                rhs_scale=rhs[1][:, rhs_cols],
+                start=start,
+                stop=stop,
+            )
+
+        def cols(i):
+            return slice(i * P, (i + 1) * P)
+
+        turned = {}
+        grouped = {}
+
+        def transposes(unit, blocks):
+            banks = []
+            for pair in range(len(blocks) // 2):
+                bank = psum.tile([P, 2, 2, P], F32, name="bank", tag="turn")
+                for a in (0, 1):
+                    words = blocks[2 * pair + a].bitcast(F32)
+                    for u in (0, 1):
+                        nc.tensor.transpose(bank[:, a, u, :], words[:, u::2], ident[:])
+                banks.append(bank)
+            turned[unit] = banks
+
+        def exits(unit):
+            banks = turned.pop(unit)
+            tile = work.tile([P, len(banks) * 2 * P, PACK], BF16, name="grouped_tile", tag=f"grouped{len(banks)}", align_bytes=64)
+            words = tile[:].rearrange("p c j -> p (c j)").bitcast(F32).rearrange("p (c u) -> p c u", u=2)
+            for b, bank in enumerate(banks):
+                nc.scalar.copy(
+                    out=words[:, b * 2 * P : (b + 1) * 2 * P, :].rearrange("p (a r) u -> p a r u", a=2),
+                    in_=bank[:].rearrange("p a u r -> p a r u"),
+                )
+            grouped[unit] = tile
+
+        def w2_product(r, lo, hi):
+            nc.vector.tensor_tensor(
+                out=scaled[r][:, lo:hi],
+                in0=byte_tiles[r][:, lo:hi].bitcast(FP8),
+                in1=scale_all[:, lo:hi],
+                op=MULT,
+            )
+
+        units = [("w", w, g) for g in range(GROUPS) for w in (0, 1)] + [("r", r) for r in range(ROW_TILES)]
+
+        def unit_blocks(unit):
+            if unit[0] == "w":
+                return [w_raw[unit[1], unit[2]][:, t, :] for t in range(PACK)]
+            return [scaled[unit[1]][:, g * K_PASS : (g + 1) * K_PASS] for g in range(GROUPS)]
+
+        def unit_op(unit):
+            return w_op[unit[1], unit[2]] if unit[0] == "w" else w2_op[unit[1]]
+
+        gate_up = {}
+        gated = {}
+        hidden = {}
+
+        def first_products(g):
+            for tok in range(TOKEN_TILES):
+                pair = []
+                for w in (0, 1):
+                    acc = psum.tile([P, PACK, P], F32, name="acc", tag="acc")
+                    for t in range(PACK):
+                        mx(acc[:, t, :], w_op[w, g], cols(t), x_op, cols(tok), True, True)
+                    pair.append(acc)
+                gate_up[g, tok] = pair
+
+        def silu(g):
+            for tok in range(TOKEN_TILES):
+                s = work.tile([P, P, PACK], F32, name="gated_tile", tag="gated", align_bytes=64)
+                nc.scalar.activation(out=s[:], in_=gate_up[g, tok][0][:].rearrange("p t n -> p n t"), func=ACT.Silu)
+                gated[g, tok] = s
+
+        def hidden_product(g, tok):
+            if tok == 0:
+                hidden[g] = work.tile([P, B, PACK], BF16, name="hidden_tile", tag="hidden", align_bytes=64)
+            nc.vector.tensor_tensor(
+                out=hidden[g][:, cols(tok), :],
+                in0=gate_up[g, tok][1][:].rearrange("p t n -> p n t"),
+                in1=gated[g, tok][:],
+                op=MULT,
+            )
+
+        parts = [(0, 4), (4, 7), (7, 8)]
+        accs = {}
+        sums = {}
+        gained = [keep.tile([P, D], F32, name=f"gained_{tok}", align_bytes=64) for tok in range(TOKEN_TILES)]
+
+        def part_of(r):
+            return [i for i, (lo, hi) in enumerate(parts) if lo <= r < hi][0]
+
+        def second_product(r):
+            part = part_of(r)
+            lo, hi = parts[part]
+            for tok in range(TOKEN_TILES):
+                if r == lo:
+                    accs[part, tok] = psum.tile([P, 4 * P], F32, name="token_acc", tag="turn" if part == 2 else "acc")
+                for g in range(GROUPS):
+                    mx(accs[part, tok][:, cols(r - lo)], h_op[g], cols(tok), w2_op[r], cols(g), g == 0, g == GROUPS - 1)
+
+        def squares(part, tok):
+            width = (parts[part][1] - parts[part][0]) * P
+            s = keep.tile([P, 1], F32, name=f"sum_{part}_{tok}")
+            nc.scalar.activation(out=square_out[:, :width], in_=accs[part, tok][:, :width], func=ACT.Square, accum_out=s[:])
+            sums[part, tok] = s
+
+        def gain_product(part, tok):
+            lo, hi = parts[part][0] * P, parts[part][1] * P
+            nc.vector.tensor_tensor(
+                out=gained[tok][:, lo:hi], in0=accs[part, tok][:, : hi - lo], in1=gain[:, lo:hi], op=MULT
+            )
+
+        partial = {}
+
+        def partial_mean(tok):
+            both = keep.tile([P, 1], F32, name=f"both_{tok}")
+            nc.gpsimd.tensor_tensor(out=both[:], in0=sums[0, tok][:], in1=sums[1, tok][:], op=ADD)
+            m = keep.tile([P, 1], F32, name=f"partial_{tok}")
+            nc.gpsimd.tensor_scalar(out=m[:], in0=both[:], scalar1=1.0 / D, scalar2=EPS, op0=MULT, op1=ADD)
+            partial[tok] = m
+
+        w2_product(0, 0, K_PASS)
+        x_blocks = [x_raw[:, tok, :] for tok in range(TOKEN_TILES)]
+        transposes("x", x_blocks)
+        exits("x")
+        w2_product(0, K_PASS, HALF)
+        w2_product(1, 0, HALF)
+        quantize(x_op, grouped.pop("x"))
+        w2_product(0, HALF, HID)
+        w2_product(1, HALF, HID)
+        fill = [(r, lo) for r in range(2, ROW_TILES) for lo in (0, HALF)]
+        for i in range(len(units) + 1):
+            if i < len(units):
+                transposes(units[i], unit_blocks(units[i]))
+                exits(units[i])
+            if i >= 1:
+                quantize(unit_op(units[i - 1]), grouped.pop(units[i - 1]))
+            g = (i - 4) // 2
+            starts_group = i >= 4 and i % 2 == 0 and g < GROUPS
+            if starts_group:
+                first_products(g)
+                silu(g)
+                hidden_product(g, 0)
+            if i >= 1 and fill:
+                r, lo = fill.pop(0)
+                w2_product(r, lo, lo + HALF)
+            if starts_group:
+                hidden_product(g, 1)
+            if i >= 5 and i % 2 == 1 and (i - 5) // 2 < GROUPS:
+                quantize(h_op[(i - 5) // 2], hidden.pop((i - 5) // 2))
+            if i == 11:
+                nc.scalar.activation(out=dummy_out[:], in_=dummy[:], func=ACT.Abs_reciprocal_sqrt, bias=1.0)
+                for half in (0, 1):
+                    bank = psum.tile([P, 4 * P], F32, name="bias_bank", tag="turn")
+                    nc.tensor.matmul(bank[:], ones[:], bias_rows[:, half * 512 : (half + 1) * 512], start=True, stop=True)
+                    nc.scalar.copy(out=bias[:, half * 512 : (half + 1) * 512], in_=bank[:])
+            if i == 12:
+                second_product(0)
+                second_product(1)
+            if i == 13:
+                second_product(2)
+                second_product(3)
+            if i == 14:
+                squares(0, 0)
+                squares(0, 1)
+                gain_product(0, 0)
+                second_product(4)
+            if i == 15:
+                gain_product(0, 1)
+                second_product(5)
+            if i == 16:
+                second_product(6)
+                second_product(7)
+        for tok in range(TOKEN_TILES):
+            squares(1, tok)
+            gain_product(1, tok)
+            partial_mean(tok)
+        rstd = []
+        for tok in range(TOKEN_TILES):
+            squares(2, tok)
+            gain_product(2, tok)
+            s = keep.tile([P, 1], F32, name=f"rstd_{tok}")
+            nc.scalar.activation(out=s[:], in_=sums[2, tok][:], func=ACT.Abs_reciprocal_sqrt, scale=1.0 / D, bias=partial[tok][:])
+            rstd.append(s)
+        for tok in range(TOKEN_TILES):
+            for half in (0, 1):
+                c = slice(half * 512, (half + 1) * 512)
+                y = work.tile([P, 512], F32, name="y", tag="y", align_bytes=64)
+                nc.vector.scalar_tensor_tensor(
+                    out=y[:], in0=gained[tok][:, c], scalar=rstd[tok][:], in1=bias[:, c], op0=MULT, op1=ADD
+                )
+                nc.sync.dma_start(out=out[tok * P : (tok + 1) * P, c], in_=y[:])

@@ -43,6 +43,7 @@ def tile_observationembeddingv2_pa_kernel(
                 w_raw[w, g] = keep.tile([P, PACK, G0], BF16, name=f"w_raw_{w}_{g}", align_bytes=64)
         byte_tiles = [keep.tile([P, HID], U8, name=f"byte_tile_{r}", align_bytes=64) for r in range(ROW_TILES)]
         scaled = [keep.tile([P, HID], BF16, name=f"scaled_{r}", align_bytes=64) for r in range(ROW_TILES)]
+        scale_cols = keep.tile([P, 2, 8], F32, name="scale_cols", align_bytes=64)
         scale_all = keep.tile([P, HID], F32, name="scale_all", align_bytes=64)
         gain = keep.tile([P, D], BF16, name="gain", align_bytes=64)
         bias_rows = keep.tile([P, D], BF16, name="bias_rows", align_bytes=64)
@@ -53,11 +54,7 @@ def tile_observationembeddingv2_pa_kernel(
         dummy_out = keep.tile([P, 1], F32, name="dummy_out")
         square_out = keep.tile([P, 512], F32, name="square_out", align_bytes=64)
 
-        def load_scale(g):
-            nc.sync.dma_start(
-                out=scale_all[:, g * K_PASS : (g + 1) * K_PASS],
-                in_=w2_g0_scale.rearrange("o k -> (o k)")[g * K_PASS : (g + 1) * K_PASS].partition_broadcast(P),
-            )
+        nc.scalar.dma_start(out=scale_cols[:], in_=w2_g0_scale.rearrange("o (h j c) -> j (o h) c", h=2, c=8))
 
         def load_bytes(r):
             nc.sync.dma_start(out=byte_tiles[r][:], in_=w2_g0_bytes[r * P : (r + 1) * P, :])
@@ -66,23 +63,19 @@ def tile_observationembeddingv2_pa_kernel(
             source = (w1_g0, w3_g0)[w][g * K_PASS : (g + 1) * K_PASS, :]
             nc.sync.dma_start(out=w_raw[w, g][:], in_=source.rearrange("(m t) k -> m t k", t=PACK))
 
-        load_scale(0)
-        load_bytes(0)
         nc.sync.dma_start(out=x_raw[:], in_=x0.rearrange("(a p) k -> p a k", p=P))
-        load_scale(1)
-        load_bytes(1)
+        load_bytes(0)
         load_w(0, 0)
-        load_scale(2)
-        load_scale(3)
+        load_bytes(1)
         load_w(1, 0)
-        load_bytes(2)
         load_w(0, 1)
+        load_bytes(2)
         load_w(1, 1)
-        load_bytes(3)
         load_w(0, 2)
+        load_bytes(3)
         load_w(1, 2)
-        load_bytes(4)
         load_w(0, 3)
+        load_bytes(4)
         load_w(1, 3)
         for r in range(5, ROW_TILES):
             load_bytes(r)
@@ -149,6 +142,16 @@ def tile_observationembeddingv2_pa_kernel(
                 )
             grouped[unit] = tile
 
+        def spread_scale(h):
+            for b in (0, 1):
+                bank = psum.tile([P, 4, P], F32, name="bank", tag="turn")
+                for c in range(4):
+                    nc.tensor.transpose(bank[:, c, :], scale_cols[:, h, 4 * b + c : 4 * b + c + 1].to_broadcast([P, P]), ident[:])
+                (nc.vector.tensor_copy if h == 0 else nc.scalar.copy)(
+                    out=scale_all[:, h * HALF : (h + 1) * HALF].rearrange("p (j c) -> p j c", c=8)[:, :, 4 * b : 4 * b + 4],
+                    in_=bank[:].rearrange("p c j -> p j c"),
+                )
+
         def w2_product(r, lo, hi):
             nc.vector.tensor_tensor(
                 out=scaled[r][:, lo:hi],
@@ -171,8 +174,8 @@ def tile_observationembeddingv2_pa_kernel(
         gated = {}
         hidden = {}
 
-        def first_products(g):
-            for tok in range(TOKEN_TILES):
+        def first_products(g, tok):
+            if True:
                 pair = []
                 for w in (0, 1):
                     acc = psum.tile([P, PACK, P], F32, name="acc", tag="acc")
@@ -181,8 +184,8 @@ def tile_observationembeddingv2_pa_kernel(
                     pair.append(acc)
                 gate_up[g, tok] = pair
 
-        def silu(g):
-            for tok in range(TOKEN_TILES):
+        def silu(g, tok):
+            if True:
                 s = work.tile([P, P, PACK], F32, name="gated_tile", tag="gated", align_bytes=64)
                 nc.scalar.activation(out=s[:], in_=gate_up[g, tok][0][:].rearrange("p t n -> p n t"), func=ACT.Silu)
                 gated[g, tok] = s
@@ -205,10 +208,10 @@ def tile_observationembeddingv2_pa_kernel(
         def part_of(r):
             return [i for i, (lo, hi) in enumerate(parts) if lo <= r < hi][0]
 
-        def second_product(r):
+        def second_product(r, toks=range(TOKEN_TILES)):
             part = part_of(r)
             lo, hi = parts[part]
-            for tok in range(TOKEN_TILES):
+            for tok in toks:
                 if r == lo:
                     accs[part, tok] = psum.tile([P, 4 * P], F32, name="token_acc", tag="turn" if part == 2 else "acc")
                 for g in range(GROUPS):
@@ -235,11 +238,12 @@ def tile_observationembeddingv2_pa_kernel(
             nc.gpsimd.tensor_scalar(out=m[:], in0=both[:], scalar1=1.0 / D, scalar2=EPS, op0=MULT, op1=ADD)
             partial[tok] = m
 
-        w2_product(0, 0, K_PASS)
+        spread_scale(0)
         x_blocks = [x_raw[:, tok, :] for tok in range(TOKEN_TILES)]
+        w2_product(0, 0, HALF)
+        spread_scale(1)
         transposes("x", x_blocks)
         exits("x")
-        w2_product(0, K_PASS, HALF)
         w2_product(1, 0, HALF)
         quantize(x_op, grouped.pop("x"))
         w2_product(0, HALF, HID)
@@ -249,55 +253,52 @@ def tile_observationembeddingv2_pa_kernel(
             if i < len(units):
                 transposes(units[i], unit_blocks(units[i]))
                 exits(units[i])
+            b = i - 3
+            if 0 <= b < 8:
+                first_products(b // 2, b % 2)
+                silu(b // 2, b % 2)
             if i >= 1:
                 quantize(unit_op(units[i - 1]), grouped.pop(units[i - 1]))
-            g = (i - 4) // 2
-            starts_group = i >= 4 and i % 2 == 0 and g < GROUPS
-            if starts_group:
-                first_products(g)
-                silu(g)
-                hidden_product(g, 0)
-            if i >= 1 and fill:
-                r, lo = fill.pop(0)
+            b = i - 4
+            if 0 <= b < 8:
+                hidden_product(b // 2, b % 2)
+            for r, lo in fill[[0, 0, 1, 1, 2, 2, 3, 3, 4, 5, 6, 8, 10, 12, 12, 12, 12][max(i - 1, 0)] : [0, 0, 1, 1, 2, 2, 3, 3, 4, 5, 6, 8, 10, 12, 12, 12, 12][i]]:
                 w2_product(r, lo, lo + HALF)
-            if starts_group:
-                hidden_product(g, 1)
-            if i >= 5 and i % 2 == 1 and (i - 5) // 2 < GROUPS:
-                quantize(h_op[(i - 5) // 2], hidden.pop((i - 5) // 2))
-            if i == 11:
+            if 0 <= b < 8 and b % 2 == 1:
+                quantize(h_op[b // 2], hidden.pop(b // 2))
+            if i == 12:
                 nc.scalar.activation(out=dummy_out[:], in_=dummy[:], func=ACT.Abs_reciprocal_sqrt, bias=1.0)
                 for half in (0, 1):
                     bank = psum.tile([P, 4 * P], F32, name="bias_bank", tag="turn")
                     nc.tensor.matmul(bank[:], ones[:], bias_rows[:, half * 512 : (half + 1) * 512], start=True, stop=True)
                     nc.scalar.copy(out=bias[:, half * 512 : (half + 1) * 512], in_=bank[:])
-            if i == 12:
+            if i == 13:
                 second_product(0)
                 second_product(1)
-            if i == 13:
                 second_product(2)
-                second_product(3)
             if i == 14:
+                second_product(3)
                 squares(0, 0)
                 squares(0, 1)
-                gain_product(0, 0)
                 second_product(4)
             if i == 15:
-                gain_product(0, 1)
+                gain_product(0, 0)
                 second_product(5)
             if i == 16:
-                second_product(6)
-                second_product(7)
-        for tok in range(TOKEN_TILES):
-            squares(1, tok)
-            gain_product(1, tok)
-            partial_mean(tok)
+                gain_product(0, 1)
+                for tok in range(TOKEN_TILES):
+                    second_product(6, [tok])
+                    second_product(7, [tok])
         rstd = []
         for tok in range(TOKEN_TILES):
+            squares(1, tok)
+            partial_mean(tok)
+            gain_product(1, tok)
             squares(2, tok)
-            gain_product(2, tok)
             s = keep.tile([P, 1], F32, name=f"rstd_{tok}")
             nc.scalar.activation(out=s[:], in_=sums[2, tok][:], func=ACT.Abs_reciprocal_sqrt, scale=1.0 / D, bias=partial[tok][:])
             rstd.append(s)
+            gain_product(2, tok)
         for tok in range(TOKEN_TILES):
             for half in (0, 1):
                 c = slice(half * 512, (half + 1) * 512)

@@ -24,6 +24,10 @@ GROUPS = HID // K_PASS
 ROW_TILES = D // P
 TOKEN_TILES = B // P
 HALF = HID // 2
+R_UNITS = [("r", part, g) for part in (0, 1) for g in range(GROUPS)]
+PARTS = [(0, 1, 2, 3), (4, 5, 6, 7)]
+PART_TAGS = ("out", "gate")
+R_PASSES = {unit: (unit[2],) for unit in R_UNITS}
 
 
 def tile_observationembeddingv2_pa_kernel(
@@ -48,13 +52,19 @@ def tile_observationembeddingv2_pa_kernel(
         gain = keep.tile([P, D], BF16, name="gain", align_bytes=64)
         bias_rows = keep.tile([P, D], BF16, name="bias_rows", align_bytes=64)
         ones = keep.tile([P, P], BF16, name="ones", align_bytes=64)
-        bias = keep.tile([P, D], F32, name="bias", align_bytes=64)
         ident = keep.tile([P, P], F32, name="ident", align_bytes=64)
         dummy = keep.tile([P, 1], F32, name="dummy")
         dummy_out = keep.tile([P, 1], F32, name="dummy_out")
         square_out = keep.tile([P, 512], F32, name="square_out", align_bytes=64)
 
         nc.scalar.dma_start(out=scale_cols[:], in_=w2_g0_scale.rearrange("o (h j c) -> j (o h) c", h=2, c=8))
+        make_identity(nc, ident[:])
+        nc.gpsimd.memset(bias_rows[:], 0.0)
+        nc.gpsimd.memset(ones[:], 1.0)
+        nc.vector.memset(dummy[:], 0.0)
+        nc.scalar.dma_start(out=bias_rows[0:1, :], in_=norm_b.rearrange("(o d) -> o d", o=1))
+        nc.scalar.dma_start(out=bias_rows[1:2, :], in_=term_embed0.rearrange("(o d) -> o d", o=1))
+        nc.scalar.activation(out=dummy_out[:], in_=dummy[:], func=ACT.Silu)
 
         def load_bytes(r):
             nc.sync.dma_start(out=byte_tiles[r][:], in_=w2_g0_bytes[r * P : (r + 1) * P, :])
@@ -63,31 +73,27 @@ def tile_observationembeddingv2_pa_kernel(
             source = (w1_g0, w3_g0)[w][g * K_PASS : (g + 1) * K_PASS, :]
             nc.sync.dma_start(out=w_raw[w, g][:], in_=source.rearrange("(m t) k -> m t k", t=PACK))
 
-        nc.sync.dma_start(out=x_raw[:], in_=x0.rearrange("(a p) k -> p a k", p=P))
+        def load_x():
+            nc.sync.dma_start(out=x_raw[:], in_=x0.rearrange("(a p) k -> p a k", p=P))
+
+        load_x()
         load_bytes(0)
-        load_w(0, 0)
         load_bytes(1)
-        load_w(1, 0)
-        load_w(0, 1)
+        load_w(0, 0)
         load_bytes(2)
+        load_w(1, 0)
+        load_bytes(3)
+        load_w(0, 1)
         load_w(1, 1)
         load_w(0, 2)
-        load_bytes(3)
         load_w(1, 2)
-        load_w(0, 3)
         load_bytes(4)
+        load_w(0, 3)
         load_w(1, 3)
-        for r in range(5, ROW_TILES):
-            load_bytes(r)
+        load_bytes(5)
+        load_bytes(6)
+        load_bytes(7)
         nc.sync.dma_start(out=gain[:], in_=norm_w.partition_broadcast(P))
-
-        make_identity(nc, ident[:])
-        nc.gpsimd.memset(bias_rows[:], 0.0)
-        nc.gpsimd.memset(ones[:], 1.0)
-        nc.vector.memset(dummy[:], 0.0)
-        nc.scalar.dma_start(out=bias_rows[0:1, :], in_=norm_b.rearrange("(o d) -> o d", o=1))
-        nc.scalar.dma_start(out=bias_rows[1:2, :], in_=term_embed0.rearrange("(o d) -> o d", o=1))
-        nc.scalar.activation(out=dummy_out[:], in_=dummy[:], func=ACT.Silu)
 
         def operand(name, width):
             return (
@@ -98,7 +104,7 @@ def tile_observationembeddingv2_pa_kernel(
         x_op = operand("x", B)
         w_op = {(w, g): operand(f"w_{w}_{g}", K_PASS) for w in (0, 1) for g in range(GROUPS)}
         h_op = [operand(f"h_{g}", B) for g in range(GROUPS)]
-        w2_op = [operand(f"w2_{r}", K_PASS) for r in range(ROW_TILES)]
+        w2_op = {unit[1:]: operand("w2_%d_%d" % unit[1:], K_PASS) for unit in R_UNITS}
 
         def quantize(op, values):
             nc.vector.quantize_mx(out=op[0][:].bitcast(FP8X4), scales=op[1][:], in_=values[:].rearrange("p c j -> p (c j)"))
@@ -131,23 +137,27 @@ def tile_observationembeddingv2_pa_kernel(
                 banks.append(bank)
             turned[unit] = banks
 
+        def group_tile(unit, width):
+            if unit not in grouped:
+                grouped[unit] = work.tile([P, width, PACK], BF16, name="grouped_tile", tag=f"grouped{width}", align_bytes=64)
+            return grouped[unit]
+
         def exits(unit):
             banks = turned.pop(unit)
-            tile = work.tile([P, len(banks) * 2 * P, PACK], BF16, name="grouped_tile", tag=f"grouped{len(banks)}", align_bytes=64)
+            tile = group_tile(unit, B if unit == "x" else K_PASS)
             words = tile[:].rearrange("p c j -> p (c j)").bitcast(F32).rearrange("p (c u) -> p c u", u=2)
             for b, bank in enumerate(banks):
                 nc.scalar.copy(
                     out=words[:, b * 2 * P : (b + 1) * 2 * P, :].rearrange("p (a r) u -> p a r u", a=2),
                     in_=bank[:].rearrange("p a u r -> p a r u"),
                 )
-            grouped[unit] = tile
 
-        def spread_scale(h):
+        def spread_scale(h, copy):
             for b in (0, 1):
                 bank = psum.tile([P, 4, P], F32, name="bank", tag="turn")
                 for c in range(4):
                     nc.tensor.transpose(bank[:, c, :], scale_cols[:, h, 4 * b + c : 4 * b + c + 1].to_broadcast([P, P]), ident[:])
-                (nc.vector.tensor_copy if h == 0 else nc.scalar.copy)(
+                copy(
                     out=scale_all[:, h * HALF : (h + 1) * HALF].rearrange("p (j c) -> p j c", c=8)[:, :, 4 * b : 4 * b + 4],
                     in_=bank[:].rearrange("p c j -> p j c"),
                 )
@@ -160,15 +170,14 @@ def tile_observationembeddingv2_pa_kernel(
                 op=MULT,
             )
 
-        units = [("w", w, g) for g in range(GROUPS) for w in (0, 1)] + [("r", r) for r in range(ROW_TILES)]
-
         def unit_blocks(unit):
             if unit[0] == "w":
                 return [w_raw[unit[1], unit[2]][:, t, :] for t in range(PACK)]
-            return [scaled[unit[1]][:, g * K_PASS : (g + 1) * K_PASS] for g in range(GROUPS)]
+            rows, passes = PARTS[unit[1]], R_PASSES[unit]
+            return [scaled[r][:, g * K_PASS : (g + 1) * K_PASS] for g in passes for r in rows]
 
         def unit_op(unit):
-            return w_op[unit[1], unit[2]] if unit[0] == "w" else w2_op[unit[1]]
+            return w_op[unit[1], unit[2]] if unit[0] == "w" else w2_op[unit[1:]]
 
         gate_up = {}
         gated = {}
@@ -178,7 +187,7 @@ def tile_observationembeddingv2_pa_kernel(
             if True:
                 pair = []
                 for w in (0, 1):
-                    acc = psum.tile([P, PACK, P], F32, name="acc", tag="acc")
+                    acc = psum.tile([P, PACK, P], F32, name="gate_bank", tag="gate", bufs=2)
                     for t in range(PACK):
                         mx(acc[:, t, :], w_op[w, g], cols(t), x_op, cols(tok), True, True)
                     pair.append(acc)
@@ -200,110 +209,209 @@ def tile_observationembeddingv2_pa_kernel(
                 op=MULT,
             )
 
-        parts = [(0, 4), (4, 7), (7, 8)]
+        def turn(unit):
+            transposes(unit, unit_blocks(unit))
+            exits(unit)
+
+        def quantize_unit(unit):
+            quantize(unit_op(unit), grouped.pop(unit))
+
+        def turn_x():
+            transposes("x", [x_raw[:, tok, :] for tok in range(TOKEN_TILES)])
+            exits("x")
+
+        def quantize_x():
+            quantize(x_op, grouped.pop("x"))
+
+        def quantize_h(g):
+            quantize(h_op[g], hidden.pop(g))
+
         accs = {}
         sums = {}
         gained = [keep.tile([P, D], F32, name=f"gained_{tok}", align_bytes=64) for tok in range(TOKEN_TILES)]
 
-        def part_of(r):
-            return [i for i, (lo, hi) in enumerate(parts) if lo <= r < hi][0]
+        def part_columns(part):
+            rows = PARTS[part]
+            return slice(rows[0] * P, (rows[-1] + 1) * P)
 
-        def second_product(r, toks=range(TOKEN_TILES)):
-            part = part_of(r)
-            lo, hi = parts[part]
-            for tok in toks:
-                if r == lo:
-                    accs[part, tok] = psum.tile([P, 4 * P], F32, name="token_acc", tag="turn" if part == 2 else "acc")
-                for g in range(GROUPS):
-                    mx(accs[part, tok][:, cols(r - lo)], h_op[g], cols(tok), w2_op[r], cols(g), g == 0, g == GROUPS - 1)
+        def second_product(unit, tok):
+            part = unit[1]
+            width = len(PARTS[part]) * P
+            for n, g in enumerate(R_PASSES[unit]):
+                if g == 0:
+                    accs[part, tok] = psum.tile([P, 4 * P], F32, name="part_bank", tag=PART_TAGS[part], bufs=4 if PART_TAGS[part] == "turn" else 2)
+                mx(accs[part, tok][:, :width], h_op[g], cols(tok), w2_op[unit[1:]], slice(n * width, (n + 1) * width), g == 0, g == GROUPS - 1)
 
         def squares(part, tok):
-            width = (parts[part][1] - parts[part][0]) * P
+            c = part_columns(part)
+            width = c.stop - c.start
             s = keep.tile([P, 1], F32, name=f"sum_{part}_{tok}")
             nc.scalar.activation(out=square_out[:, :width], in_=accs[part, tok][:, :width], func=ACT.Square, accum_out=s[:])
             sums[part, tok] = s
 
         def gain_product(part, tok):
-            lo, hi = parts[part][0] * P, parts[part][1] * P
+            c = part_columns(part)
             nc.vector.tensor_tensor(
-                out=gained[tok][:, lo:hi], in0=accs[part, tok][:, : hi - lo], in1=gain[:, lo:hi], op=MULT
+                out=gained[tok][:, c], in0=accs[part, tok][:, : c.stop - c.start], in1=gain[:, c], op=MULT
             )
 
         partial = {}
 
         def partial_mean(tok):
-            both = keep.tile([P, 1], F32, name=f"both_{tok}")
-            nc.gpsimd.tensor_tensor(out=both[:], in0=sums[0, tok][:], in1=sums[1, tok][:], op=ADD)
+            total = sums[0, tok]
+            for part in range(1, len(PARTS) - 1):
+                both = keep.tile([P, 1], F32, name=f"both_{part}_{tok}")
+                nc.gpsimd.tensor_tensor(out=both[:], in0=total[:], in1=sums[part, tok][:], op=ADD)
+                total = both
             m = keep.tile([P, 1], F32, name=f"partial_{tok}")
-            nc.gpsimd.tensor_scalar(out=m[:], in0=both[:], scalar1=1.0 / D, scalar2=EPS, op0=MULT, op1=ADD)
+            nc.gpsimd.tensor_scalar(out=m[:], in0=total[:], scalar1=1.0 / D, scalar2=EPS, op0=MULT, op1=ADD)
             partial[tok] = m
 
-        spread_scale(0)
-        x_blocks = [x_raw[:, tok, :] for tok in range(TOKEN_TILES)]
-        w2_product(0, 0, HALF)
-        spread_scale(1)
-        transposes("x", x_blocks)
-        exits("x")
-        w2_product(1, 0, HALF)
-        quantize(x_op, grouped.pop("x"))
-        w2_product(0, HALF, HID)
-        w2_product(1, HALF, HID)
-        fill = [(r, lo) for r in range(2, ROW_TILES) for lo in (0, HALF)]
-        for i in range(len(units) + 1):
-            if i < len(units):
-                transposes(units[i], unit_blocks(units[i]))
-                exits(units[i])
-            b = i - 3
-            if 0 <= b < 8:
-                first_products(b // 2, b % 2)
-                silu(b // 2, b % 2)
-            if i >= 1:
-                quantize(unit_op(units[i - 1]), grouped.pop(units[i - 1]))
-            b = i - 4
-            if 0 <= b < 8:
-                hidden_product(b // 2, b % 2)
-            for r, lo in fill[[0, 0, 1, 1, 2, 2, 3, 3, 4, 5, 6, 8, 10, 12, 12, 12, 12][max(i - 1, 0)] : [0, 0, 1, 1, 2, 2, 3, 3, 4, 5, 6, 8, 10, 12, 12, 12, 12][i]]:
-                w2_product(r, lo, lo + HALF)
-            if 0 <= b < 8 and b % 2 == 1:
-                quantize(h_op[b // 2], hidden.pop(b // 2))
-            if i == 12:
-                nc.scalar.activation(out=dummy_out[:], in_=dummy[:], func=ACT.Abs_reciprocal_sqrt, bias=1.0)
-                for half in (0, 1):
-                    bank = psum.tile([P, 4 * P], F32, name="bias_bank", tag="turn")
-                    nc.tensor.matmul(bank[:], ones[:], bias_rows[:, half * 512 : (half + 1) * 512], start=True, stop=True)
-                    nc.scalar.copy(out=bias[:, half * 512 : (half + 1) * 512], in_=bank[:])
-            if i == 13:
-                second_product(0)
-                second_product(1)
-                second_product(2)
-            if i == 14:
-                second_product(3)
-                squares(0, 0)
-                squares(0, 1)
-                second_product(4)
-            if i == 15:
-                gain_product(0, 0)
-                second_product(5)
-            if i == 16:
-                gain_product(0, 1)
-                for tok in range(TOKEN_TILES):
-                    second_product(6, [tok])
-                    second_product(7, [tok])
-        rstd = []
-        for tok in range(TOKEN_TILES):
-            squares(1, tok)
-            partial_mean(tok)
-            gain_product(1, tok)
-            squares(2, tok)
+        rstd = {}
+
+        def reciprocal_root(tok):
             s = keep.tile([P, 1], F32, name=f"rstd_{tok}")
-            nc.scalar.activation(out=s[:], in_=sums[2, tok][:], func=ACT.Abs_reciprocal_sqrt, scale=1.0 / D, bias=partial[tok][:])
-            rstd.append(s)
-            gain_product(2, tok)
-        for tok in range(TOKEN_TILES):
+            nc.scalar.activation(
+                out=s[:], in_=sums[len(PARTS) - 1, tok][:], func=ACT.Abs_reciprocal_sqrt, scale=1.0 / D, bias=partial[tok][:]
+            )
+            rstd[tok] = s
+
+        def finish(tok, lo, hi):
+            y = work.tile([P, 512], F32, name="y", tag="y", align_bytes=64)
+            half, first = divmod(lo, 512)
+            nc.vector.scalar_tensor_tensor(
+                out=y[:, : hi - lo],
+                in0=gained[tok][:, lo:hi],
+                scalar=rstd[tok][:],
+                in1=bias_banks[half][:, first : first + hi - lo],
+                op0=MULT,
+                op1=ADD,
+            )
+            nc.sync.dma_start(out=out[tok * P : (tok + 1) * P, lo:hi], in_=y[:, : hi - lo])
+
+        def load_root_table():
+            nc.scalar.activation(out=dummy_out[:], in_=dummy[:], func=ACT.Abs_reciprocal_sqrt, bias=1.0)
+
+        bias_banks = []
+
+        def spread_bias():
             for half in (0, 1):
-                c = slice(half * 512, (half + 1) * 512)
-                y = work.tile([P, 512], F32, name="y", tag="y", align_bytes=64)
-                nc.vector.scalar_tensor_tensor(
-                    out=y[:], in0=gained[tok][:, c], scalar=rstd[tok][:], in1=bias[:, c], op0=MULT, op1=ADD
-                )
-                nc.sync.dma_start(out=out[tok * P : (tok + 1) * P, c], in_=y[:])
+                bank = psum.tile([P, 4 * P], F32, name="bias_bank", tag="turn")
+                nc.tensor.matmul(bank[:], ones[:], bias_rows[:, half * 512 : (half + 1) * 512], start=True, stop=True)
+                bias_banks.append(bank)
+
+        spread_scale(0, nc.vector.tensor_copy)
+        w2_product(0, 0, HALF)
+        spread_scale(1, nc.scalar.copy)
+        turn_x()
+        w2_product(1, 0, HALF)
+        quantize_x()
+        w2_product(2, 0, HALF)
+        w2_product(3, 0, HALF)
+        turn(("w", 0, 0))
+        turn(("w", 1, 0))
+        w2_product(0, HALF, HID)
+        turn(("r", 0, 0))
+        quantize_unit(("w", 0, 0))
+        w2_product(1, HALF, HID)
+        turn(("w", 0, 1))
+        quantize_unit(("w", 1, 0))
+        w2_product(2, HALF, HID)
+        turn(("w", 1, 1))
+        first_products(0, 0)
+        silu(0, 0)
+        quantize_unit(("r", 0, 0))
+        w2_product(3, HALF, HID)
+        turn(("r", 0, 1))
+        hidden_product(0, 0)
+        first_products(0, 1)
+        silu(0, 1)
+        quantize_unit(("w", 0, 1))
+        w2_product(4, 0, HALF)
+        turn(("w", 0, 2))
+        hidden_product(0, 1)
+        quantize_unit(("w", 1, 1))
+        w2_product(5, 0, HALF)
+        quantize_h(0)
+        turn(("w", 1, 2))
+        first_products(1, 0)
+        silu(1, 0)
+        quantize_unit(("r", 0, 1))
+        w2_product(6, 0, HALF)
+        turn(("r", 0, 2))
+        hidden_product(1, 0)
+        first_products(1, 1)
+        silu(1, 1)
+        quantize_unit(("w", 0, 2))
+        w2_product(7, 0, HALF)
+        turn(("w", 0, 3))
+        hidden_product(1, 1)
+        quantize_unit(("w", 1, 2))
+        w2_product(4, HALF, HID)
+        quantize_h(1)
+        second_product(("r", 0, 0), 0)
+        second_product(("r", 0, 0), 1)
+        turn(("w", 1, 3))
+        first_products(2, 0)
+        silu(2, 0)
+        quantize_unit(("r", 0, 2))
+        w2_product(5, HALF, HID)
+        turn(("r", 0, 3))
+        hidden_product(2, 0)
+        first_products(2, 1)
+        silu(2, 1)
+        quantize_unit(("w", 0, 3))
+        w2_product(6, HALF, HID)
+        turn(("r", 1, 0))
+        hidden_product(2, 1)
+        quantize_unit(("w", 1, 3))
+        w2_product(7, HALF, HID)
+        quantize_h(2)
+        second_product(("r", 0, 1), 0)
+        second_product(("r", 0, 1), 1)
+        turn(("r", 1, 1))
+        first_products(3, 0)
+        silu(3, 0)
+        quantize_unit(("r", 0, 3))
+        turn(("r", 1, 2))
+        hidden_product(3, 0)
+        first_products(3, 1)
+        silu(3, 1)
+        quantize_unit(("r", 1, 0))
+        load_root_table()
+        turn(("r", 1, 3))
+        hidden_product(3, 1)
+        quantize_unit(("r", 1, 1))
+        quantize_h(3)
+        second_product(("r", 0, 2), 0)
+        second_product(("r", 0, 2), 1)
+        quantize_unit(("r", 1, 2))
+        quantize_unit(("r", 1, 3))
+        second_product(("r", 0, 3), 0)
+        second_product(("r", 0, 3), 1)
+        second_product(("r", 1, 0), 0)
+        second_product(("r", 1, 0), 1)
+        second_product(("r", 1, 1), 0)
+        second_product(("r", 1, 1), 1)
+        second_product(("r", 1, 2), 0)
+        second_product(("r", 1, 2), 1)
+        second_product(("r", 1, 3), 0)
+        second_product(("r", 1, 3), 1)
+        squares(0, 0)
+        squares(0, 1)
+        gain_product(0, 0)
+        gain_product(0, 1)
+        spread_bias()
+        partial_mean(0)
+        partial_mean(1)
+        gain_product(1, 1)
+        squares(1, 0)
+        squares(1, 1)
+        gain_product(1, 0)
+        reciprocal_root(0)
+        reciprocal_root(1)
+        finish(0, 0, 512)
+        finish(0, 512, 1024)
+        finish(1, 0, 512)
+        finish(1, 512, 768)
+        finish(1, 768, 1024)

from contextlib import ExitStack

import concourse.mybir as mybir
from concourse.masks import make_identity

B, G0, HID, D = 256, 512, 2048, 1024
EPS = 1e-5
FLOPS = 2 * B * G0 * HID * 2 + 2 * B * HID * D

F32 = mybir.dt.float32
BF16 = mybir.dt.bfloat16
U32 = mybir.dt.uint32
U8 = mybir.dt.uint8
FP8 = mybir.dt.float8_e4m3fn
FP8X4 = mybir.dt.float8_e4m3fn_x4
MULT = mybir.AluOpType.mult
ADD = mybir.AluOpType.add
ACT = mybir.ActivationFunctionType

P = 128
PACK = 4
K_PASS = P * PACK
GROUPS = HID // K_PASS
ROW_TILES = D // P
TOKEN_TILES = B // P
HALF = HID // 2
R_UNITS = [("r", part, g) for part in (0, 1) for g in range(GROUPS)]
PARTS = [(0, 1, 2, 3), (4, 5, 6, 7)]
PART_TAGS = ("out", "gate")
R_PASSES = {unit: (unit[2],) for unit in R_UNITS}


def tile_observationembeddingv2_pa_kernel(
    tc, x0, w1_g0, w3_g0, w2_g0_bytes, w2_g0_scale, norm_w, norm_b, term_embed0, out
):
    nc = tc.nc
    with ExitStack() as ctx:
        keep = ctx.enter_context(tc.tile_pool(name="keep", bufs=1))
        work = ctx.enter_context(tc.tile_pool(name="work", bufs=6))
        psum = ctx.enter_context(tc.psum_pool(name="psum", bufs=4))
        ctx.enter_context(tc.manual_schedule())

        x_raw = keep.tile([P, TOKEN_TILES, G0], BF16, name="x_raw", align_bytes=64)
        w_raw = {}
        for g in range(GROUPS):
            for w in (0, 1):
                w_raw[w, g] = keep.tile([P, PACK, G0], BF16, name=f"w_raw_{w}_{g}", align_bytes=64)
        byte_tiles = [keep.tile([P, HID], U8, name=f"byte_tile_{r}", align_bytes=64) for r in range(ROW_TILES)]
        scaled = [keep.tile([P, HID], BF16, name=f"scaled_{r}", align_bytes=64) for r in range(ROW_TILES)]
        scale_cols = keep.tile([P, 2, 8], F32, name="scale_cols", align_bytes=64)
        scale_all = keep.tile([P, HID], F32, name="scale_all", align_bytes=64)
        gain = keep.tile([P, D], BF16, name="gain", align_bytes=64)
        bias_rows = keep.tile([P, D], BF16, name="bias_rows", align_bytes=64)
        ones = keep.tile([P, P], BF16, name="ones", align_bytes=64)
        ident = keep.tile([P, P], F32, name="ident", align_bytes=64)
        dummy = keep.tile([P, 1], F32, name="dummy")
        dummy_out = keep.tile([P, 1], F32, name="dummy_out")
        square_out = keep.tile([P, 512], F32, name="square_out", align_bytes=64)

        nc.scalar.dma_start(out=scale_cols[:], in_=w2_g0_scale.rearrange("o (h j c) -> j (o h) c", h=2, c=8))
        make_identity(nc, ident[:])
        nc.gpsimd.memset(bias_rows[:], 0.0)
        nc.gpsimd.memset(ones[:], 1.0)
        nc.vector.memset(dummy[:], 0.0)
        nc.scalar.dma_start(out=bias_rows[0:1, :], in_=norm_b.rearrange("(o d) -> o d", o=1))
        nc.scalar.dma_start(out=bias_rows[1:2, :], in_=term_embed0.rearrange("(o d) -> o d", o=1))
        nc.scalar.activation(out=dummy_out[:], in_=dummy[:], func=ACT.Silu)

        def load_bytes(r):
            nc.sync.dma_start(out=byte_tiles[r][:], in_=w2_g0_bytes[r * P : (r + 1) * P, :])

        def load_w(w, g):
            source = (w1_g0, w3_g0)[w][g * K_PASS : (g + 1) * K_PASS, :]
            nc.sync.dma_start(out=w_raw[w, g][:], in_=source.rearrange("(m t) k -> m t k", t=PACK))

        def load_x():
            nc.sync.dma_start(out=x_raw[:], in_=x0.rearrange("(a p) k -> p a k", p=P))

        load_x()
        load_bytes(0)
        load_bytes(1)
        load_w(0, 0)
        load_bytes(2)
        load_w(1, 0)
        load_bytes(3)
        load_w(0, 1)
        load_w(1, 1)
        load_w(0, 2)
        load_w(1, 2)
        load_bytes(4)
        load_w(0, 3)
        load_w(1, 3)
        load_bytes(5)
        load_bytes(6)
        load_bytes(7)
        nc.sync.dma_start(out=gain[:], in_=norm_w.partition_broadcast(P))

        def operand(name, width):
            return (
                keep.tile([P, width], U32, name=name + "_codes", align_bytes=64),
                keep.tile([P, width], U8, name=name + "_scales", align_bytes=64),
            )

        x_op = operand("x", B)
        w_op = {(w, g): operand(f"w_{w}_{g}", K_PASS) for w in (0, 1) for g in range(GROUPS)}
        h_op = [operand(f"h_{g}", B) for g in range(GROUPS)]
        w2_op = {unit[1:]: operand("w2_%d_%d" % unit[1:], K_PASS) for unit in R_UNITS}

        def quantize(op, values):
            nc.vector.quantize_mx(out=op[0][:].bitcast(FP8X4), scales=op[1][:], in_=values[:].rearrange("p c j -> p (c j)"))

        def mx(acc, lhs, lhs_cols, rhs, rhs_cols, start, stop):
            nc.tensor.matmul_mx(
                out=acc,
                lhsT=lhs[0][:, lhs_cols].bitcast(FP8X4),
                lhsT_scale=lhs[1][:, lhs_cols],
                rhs=rhs[0][:, rhs_cols].bitcast(FP8X4),
                rhs_scale=rhs[1][:, rhs_cols],
                start=start,
                stop=stop,
            )

        def cols(i):
            return slice(i * P, (i + 1) * P)

        turned = {}
        grouped = {}

        def transposes(unit, blocks):
            banks = []
            for pair in range(len(blocks) // 2):
                bank = psum.tile([P, 2, 2, P], F32, name="bank", tag="turn")
                for a in (0, 1):
                    words = blocks[2 * pair + a].bitcast(F32)
                    for u in (0, 1):
                        nc.tensor.transpose(bank[:, a, u, :], words[:, u::2], ident[:])
                banks.append(bank)
            turned[unit] = banks

        def group_tile(unit, width):
            if unit not in grouped:
                grouped[unit] = work.tile([P, width, PACK], BF16, name="grouped_tile", tag=f"grouped{width}", align_bytes=64)
            return grouped[unit]

        def exits(unit):
            banks = turned.pop(unit)
            tile = group_tile(unit, B if unit == "x" else K_PASS)
            words = tile[:].rearrange("p c j -> p (c j)").bitcast(F32).rearrange("p (c u) -> p c u", u=2)
            for b, bank in enumerate(banks):
                nc.scalar.copy(
                    out=words[:, b * 2 * P : (b + 1) * 2 * P, :].rearrange("p (a r) u -> p a r u", a=2),
                    in_=bank[:].rearrange("p a u r -> p a r u"),
                )

        def spread_scale(h, copy):
            for b in (0, 1):
                bank = psum.tile([P, 4, P], F32, name="bank", tag="turn")
                for c in range(4):
                    nc.tensor.transpose(bank[:, c, :], scale_cols[:, h, 4 * b + c : 4 * b + c + 1].to_broadcast([P, P]), ident[:])
                copy(
                    out=scale_all[:, h * HALF : (h + 1) * HALF].rearrange("p (j c) -> p j c", c=8)[:, :, 4 * b : 4 * b + 4],
                    in_=bank[:].rearrange("p c j -> p j c"),
                )

        def w2_product(r, lo, hi):
            nc.vector.tensor_tensor(
                out=scaled[r][:, lo:hi],
                in0=byte_tiles[r][:, lo:hi].bitcast(FP8),
                in1=scale_all[:, lo:hi],
                op=MULT,
            )

        def unit_blocks(unit):
            if unit[0] == "w":
                return [w_raw[unit[1], unit[2]][:, t, :] for t in range(PACK)]
            rows, passes = PARTS[unit[1]], R_PASSES[unit]
            return [scaled[r][:, g * K_PASS : (g + 1) * K_PASS] for g in passes for r in rows]

        def unit_op(unit):
            return w_op[unit[1], unit[2]] if unit[0] == "w" else w2_op[unit[1:]]

        gate_up = {}
        gated = {}
        hidden = {}

        def first_products(g, tok):
            if True:
                pair = []
                for w in (0, 1):
                    acc = psum.tile([P, PACK, P], F32, name="gate_bank", tag="gate", bufs=2)
                    for t in range(PACK):
                        mx(acc[:, t, :], w_op[w, g], cols(t), x_op, cols(tok), True, True)
                    pair.append(acc)
                gate_up[g, tok] = pair

        def silu(g, tok):
            if True:
                s = work.tile([P, P, PACK], F32, name="gated_tile", tag="gated", align_bytes=64)
                nc.scalar.activation(out=s[:], in_=gate_up[g, tok][0][:].rearrange("p t n -> p n t"), func=ACT.Silu)
                gated[g, tok] = s

        def hidden_product(g, tok):
            if tok == 0:
                hidden[g] = work.tile([P, B, PACK], BF16, name="hidden_tile", tag="hidden", align_bytes=64)
            nc.vector.tensor_tensor(
                out=hidden[g][:, cols(tok), :],
                in0=gate_up[g, tok][1][:].rearrange("p t n -> p n t"),
                in1=gated[g, tok][:],
                op=MULT,
            )

        def turn(unit):
            transposes(unit, unit_blocks(unit))
            exits(unit)

        def quantize_unit(unit):
            quantize(unit_op(unit), grouped.pop(unit))

        def turn_x():
            transposes("x", [x_raw[:, tok, :] for tok in range(TOKEN_TILES)])
            exits("x")

        def quantize_x():
            quantize(x_op, grouped.pop("x"))

        def quantize_h(g):
            quantize(h_op[g], hidden.pop(g))

        accs = {}
        sums = {}
        gained = [keep.tile([P, D], F32, name=f"gained_{tok}", align_bytes=64) for tok in range(TOKEN_TILES)]

        def part_columns(part):
            rows = PARTS[part]
            return slice(rows[0] * P, (rows[-1] + 1) * P)

        def second_product(unit, tok):
            part = unit[1]
            width = len(PARTS[part]) * P
            for n, g in enumerate(R_PASSES[unit]):
                if g == 0:
                    accs[part, tok] = psum.tile([P, 4 * P], F32, name="part_bank", tag=PART_TAGS[part], bufs=4 if PART_TAGS[part] == "turn" else 2)
                mx(accs[part, tok][:, :width], h_op[g], cols(tok), w2_op[unit[1:]], slice(n * width, (n + 1) * width), g == 0, g == GROUPS - 1)

        def squares(part, tok):
            c = part_columns(part)
            width = c.stop - c.start
            s = keep.tile([P, 1], F32, name=f"sum_{part}_{tok}")
            nc.scalar.activation(out=square_out[:, :width], in_=accs[part, tok][:, :width], func=ACT.Square, accum_out=s[:])
            sums[part, tok] = s

        def gain_product(part, tok):
            c = part_columns(part)
            nc.vector.tensor_tensor(
                out=gained[tok][:, c], in0=accs[part, tok][:, : c.stop - c.start], in1=gain[:, c], op=MULT
            )

        partial = {}

        def partial_mean(tok):
            total = sums[0, tok]
            for part in range(1, len(PARTS) - 1):
                both = keep.tile([P, 1], F32, name=f"both_{part}_{tok}")
                nc.gpsimd.tensor_tensor(out=both[:], in0=total[:], in1=sums[part, tok][:], op=ADD)
                total = both
            m = keep.tile([P, 1], F32, name=f"partial_{tok}")
            nc.gpsimd.tensor_scalar(out=m[:], in0=total[:], scalar1=1.0 / D, scalar2=EPS, op0=MULT, op1=ADD)
            partial[tok] = m

        rstd = {}

        def reciprocal_root(tok):
            s = keep.tile([P, 1], F32, name=f"rstd_{tok}")
            nc.scalar.activation(
                out=s[:], in_=sums[len(PARTS) - 1, tok][:], func=ACT.Abs_reciprocal_sqrt, scale=1.0 / D, bias=partial[tok][:]
            )
            rstd[tok] = s

        def finish(tok, lo, hi):
            y = work.tile([P, 512], F32, name="y", tag="y", align_bytes=64)
            half, first = divmod(lo, 512)
            nc.vector.scalar_tensor_tensor(
                out=y[:, : hi - lo],
                in0=gained[tok][:, lo:hi],
                scalar=rstd[tok][:],
                in1=bias_banks[half][:, first : first + hi - lo],
                op0=MULT,
                op1=ADD,
            )
            nc.sync.dma_start(out=out[tok * P : (tok + 1) * P, lo:hi], in_=y[:, : hi - lo])

        def load_root_table():
            nc.scalar.activation(out=dummy_out[:], in_=dummy[:], func=ACT.Abs_reciprocal_sqrt, bias=1.0)

        bias_banks = []

        def spread_bias():
            for half in (0, 1):
                bank = psum.tile([P, 4 * P], F32, name="bias_bank", tag="turn")
                nc.tensor.matmul(bank[:], ones[:], bias_rows[:, half * 512 : (half + 1) * 512], start=True, stop=True)
                bias_banks.append(bank)

        spread_scale(0, nc.vector.tensor_copy)
        w2_product(0, 0, HALF)
        spread_scale(1, nc.scalar.copy)
        turn_x()
        w2_product(1, 0, HALF)
        quantize_x()
        w2_product(2, 0, HALF)
        w2_product(3, 0, HALF)
        turn(("w", 0, 0))
        turn(("w", 1, 0))
        w2_product(0, HALF, HID)
        turn(("r", 0, 0))
        quantize_unit(("w", 0, 0))
        w2_product(1, HALF, HID)
        turn(("w", 0, 1))
        quantize_unit(("w", 1, 0))
        w2_product(2, HALF, HID)
        turn(("w", 1, 1))
        first_products(0, 0)
        silu(0, 0)
        quantize_unit(("r", 0, 0))
        w2_product(3, HALF, HID)
        turn(("r", 0, 1))
        hidden_product(0, 0)
        first_products(0, 1)
        silu(0, 1)
        quantize_unit(("w", 0, 1))
        w2_product(4, 0, HALF)
        turn(("w", 0, 2))
        hidden_product(0, 1)
        quantize_unit(("w", 1, 1))
        w2_product(5, 0, HALF)
        quantize_h(0)
        turn(("w", 1, 2))
        first_products(1, 0)
        silu(1, 0)
        quantize_unit(("r", 0, 1))
        w2_product(6, 0, HALF)
        turn(("r", 0, 2))
        hidden_product(1, 0)
        first_products(1, 1)
        silu(1, 1)
        quantize_unit(("w", 0, 2))
        w2_product(7, 0, HALF)
        turn(("w", 0, 3))
        hidden_product(1, 1)
        quantize_unit(("w", 1, 2))
        w2_product(4, HALF, HID)
        quantize_h(1)
        second_product(("r", 0, 0), 0)
        second_product(("r", 0, 0), 1)
        turn(("w", 1, 3))
        first_products(2, 0)
        silu(2, 0)
        quantize_unit(("r", 0, 2))
        w2_product(5, HALF, HID)
        turn(("r", 0, 3))
        hidden_product(2, 0)
        first_products(2, 1)
        silu(2, 1)
        quantize_unit(("w", 0, 3))
        w2_product(6, HALF, HID)
        turn(("r", 1, 0))
        hidden_product(2, 1)
        quantize_unit(("w", 1, 3))
        w2_product(7, HALF, HID)
        quantize_h(2)
        second_product(("r", 0, 1), 0)
        second_product(("r", 0, 1), 1)
        turn(("r", 1, 1))
        first_products(3, 0)
        silu(3, 0)
        quantize_unit(("r", 0, 3))
        turn(("r", 1, 2))
        hidden_product(3, 0)
        first_products(3, 1)
        silu(3, 1)
        quantize_unit(("r", 1, 0))
        load_root_table()
        turn(("r", 1, 3))
        hidden_product(3, 1)
        quantize_unit(("r", 1, 1))
        quantize_h(3)
        second_product(("r", 0, 2), 0)
        second_product(("r", 0, 2), 1)
        quantize_unit(("r", 1, 2))
        quantize_unit(("r", 1, 3))
        second_product(("r", 0, 3), 0)
        second_product(("r", 0, 3), 1)
        second_product(("r", 1, 0), 0)
        second_product(("r", 1, 0), 1)
        second_product(("r", 1, 1), 0)
        second_product(("r", 1, 1), 1)
        second_product(("r", 1, 2), 0)
        second_product(("r", 1, 2), 1)
        second_product(("r", 1, 3), 0)
        second_product(("r", 1, 3), 1)
        squares(0, 0)
        squares(0, 1)
        gain_product(0, 0)
        gain_product(0, 1)
        spread_bias()
        partial_mean(0)
        partial_mean(1)
        gain_product(1, 1)
        squares(1, 0)
        squares(1, 1)
        gain_product(1, 0)
        reciprocal_root(0)
        reciprocal_root(1)
        finish(0, 0, 512)
        finish(0, 512, 1024)
        finish(1, 0, 512)
        finish(1, 512, 768)
        finish(1, 768, 1024)
